import numpy as np
import ml_dtypes


def mxq(x, axis, fmt="e4m3"):
    dtype, down = {"e4m3": (ml_dtypes.float8_e4m3fn, 7), "e5m2": (ml_dtypes.float8_e5m2, 14)}[fmt]
    v = np.moveaxis(np.asarray(x, np.float32).astype(ml_dtypes.bfloat16).astype(np.float64), axis, -1)
    blocks = v.reshape(v.shape[:-1] + (-1, 32))
    amax = np.abs(blocks).max(-1, keepdims=True)
    byte = np.maximum(np.where(amax > 0, np.frexp(amax)[1] - 1 + 127, 0) - down, 1)
    scale = np.exp2(byte - 127.0)
    codes = (blocks / scale).astype(np.float32).astype(dtype).astype(np.float64)
    return np.moveaxis((codes * scale).reshape(v.shape), -1, axis)


WIDE = False


def mx_kscale(k):
    if not WIDE:
        return np.ones(k)
    levels = np.array([10, -10, 5, -5, 0])
    a = np.random.permutation(np.resize(levels, k // 512 * 4)).reshape(k // 512, 4)
    idx = np.arange(k)
    return np.exp2(a[idx // 512, idx % 128 // 32])


BF16 = ml_dtypes.bfloat16


def bf(x):
    return np.asarray(x, np.float32).astype(BF16)


def f64(x):
    return np.asarray(x).astype(np.float64)


B, Hh, Ww, NB, BS, ORI, RI = 4, 4, 4, 4, 512, 6, 2
C = NB * BS
R = B * ORI * Hh * Ww


def setup_inputs():
    s = mx_kscale(C)
    sb = s.reshape(NB, BS)
    t = mx_kscale(C).reshape(NB, BS)
    return {
        "xh": bf(np.random.standard_normal((B, C, ORI, Hh, Ww, RI)) * s[None, :, None, None, None, None]),
        "w1": bf(np.random.standard_normal((RI, NB, BS, BS)) / np.sqrt(RI * BS) / sb[None, :, :, None] * t[None, :, None, :]),
        "w2": bf(np.random.standard_normal((RI, NB, BS, BS)) / np.sqrt(BS) / t[None, :, :, None]),
        "b1": bf(np.random.standard_normal((RI, NB, BS)) * 0.3 * t[None, :, :]),
        "b2": bf(np.random.standard_normal((RI, NB, BS)) * 0.3),
    }


def reference(xh, w1, w2, b1, b2):
    x = f64(xh).transpose(5, 0, 2, 3, 4, 1).reshape(RI, R, NB, BS).transpose(0, 2, 1, 3)
    xq = mxq(x, 3, "e4m3")
    xr, xi = xq[0], xq[1]
    w1q = mxq(f64(w1), 2, "e4m3")
    w2q = mxq(f64(w2), 2, "e4m3")
    b1f = f64(b1)[:, :, None, :]
    b2f = f64(b2)[:, :, None, :]
    r1 = np.maximum((xr @ w1q[0]) - (xi @ w1q[1]) + b1f[0], 0.0)
    i1 = np.maximum((xr @ w1q[1]) + (xi @ w1q[0]) + b1f[1], 0.0)
    r1q = mxq(r1, 2, "e4m3")
    i1q = mxq(i1, 2, "e4m3")
    r2 = (r1q @ w2q[0]) - (i1q @ w2q[1]) + b2f[0]
    i2 = (r1q @ w2q[1]) + (i1q @ w2q[0]) + b2f[1]
    y = np.stack([r2, i2], axis=-1)
    y = y.transpose(1, 0, 2, 3).reshape(B, ORI, Hh, Ww, C, RI)
    return y.transpose(0, 4, 1, 2, 3, 5)

@@ -1,0 +1,212 @@
+import concourse.mybir as mybir
+from concourse.masks import make_identity
+
+FLOPS = 8 * 4 * 384 * 512 * 512 * 2
+
+BF16 = mybir.dt.bfloat16
+F32 = mybir.dt.float32
+U32 = mybir.dt.uint32
+U8 = mybir.dt.uint8
+FP8X4 = mybir.dt.float8_e4m3fn_x4
+RELU = mybir.ActivationFunctionType.Relu
+ADD = mybir.AluOpType.add
+
+P = 128
+PACK = 4
+BATCH = 4
+BLOCKS = 4
+WIDTH = 512
+TILES = WIDTH // P
+SPOTS = 96
+POSITIONS = BATCH * SPOTS
+PARTS = 2
+
+NEG, RE, IM = 0, POSITIONS, 2 * POSITIONS
+SETS = 3 * POSITIONS
+MOVING = ((RE, NEG), (IM, RE))
+POSITION_RANGES = ((0, 256), (256, 128))
+QUANTISE_RANGES = ((0, 1024), (1024, 128))
+
+
+def quantise_sets(nc, grouped, codes, scales):
+    for first, count in QUANTISE_RANGES:
+        nc.vector.quantize_mx(
+            out=codes[:, first : first + count].bitcast(FP8X4),
+            scales=scales[:, first : first + count],
+            in_=grouped[:, first : first + count, :].rearrange("p c j -> p (c j)"),
+        )
+
+
+def complex_product(nc, acc, w_codes, w_scales, tile_index, a_codes, a_scales, part, first, count):
+    columns = slice(tile_index * P, (tile_index + 1) * P)
+    for w_part in range(PARTS):
+        start = MOVING[part][w_part] + first
+        nc.tensor.matmul_mx(
+            out=acc,
+            lhsT=w_codes[:, w_part, columns].bitcast(FP8X4),
+            lhsT_scale=w_scales[:, w_part, columns],
+            rhs=a_codes[:, start : start + count].bitcast(FP8X4),
+            rhs_scale=a_scales[:, start : start + count],
+            start=(w_part == 0),
+            stop=(w_part == PARTS - 1),
+        )
+
+
+def tile_scatteringmodule_pa_kernel(tc, xh, w1, w2, b1, b2, out):
+    nc = tc.nc
+    x_view = xh.rearrange("b (n p j) o h w r -> n p b (j o h w r)", n=BLOCKS, p=P, j=PACK)
+    out_view = out.rearrange("b (n t p) o h w r -> n t p b (o h w r)", n=BLOCKS, t=TILES, p=P)
+
+    with (
+        tc.tile_pool(name="const", bufs=1) as const,
+        tc.tile_pool(name="raw", bufs=1) as raw,
+        tc.tile_pool(name="weights", bufs=1) as weights,
+        tc.tile_pool(name="stage", bufs=2) as stage,
+        tc.tile_pool(name="w_stage", bufs=3) as w_stage,
+        tc.tile_pool(name="results", bufs=4) as results,
+        tc.psum_pool(name="psum_hidden", bufs=4) as psum_hidden,
+        tc.psum_pool(name="psum_out", bufs=4) as psum_out,
+    ):
+        x_raw = {}
+        w_raw = {}
+        x_mx = {}
+        w_mx = {}
+        planes = {}
+        h_mx = {}
+
+        def load_x(n):
+            x_raw[n] = raw.tile([P, BATCH, PACK, SPOTS, PARTS], BF16, name="x_raw%d" % n)
+            nc.sync.dma_start(out=x_raw[n][:].rearrange("p b j q r -> p b (j q r)"), in_=x_view[n])
+
+        def load_weights(layer, n):
+            for part in range(PARTS):
+                w_tile = raw.tile([P, PACK, WIDTH], BF16, name="w_raw%d_%d_%d" % (layer, n, part))
+                if layer == 1:
+                    source = w1[part, n].rearrange("(p j) k -> p j k", j=PACK)
+                else:
+                    source = w2[part, n].rearrange("(t p) k -> p t k", p=P)
+                nc.sync.dma_start(out=w_tile[:], in_=source)
+                w_raw[(layer, n, part)] = w_tile
+
+        def prepare_x(n):
+            grouped = stage.tile([P, SETS, PACK], BF16, name="x_grouped", align_bytes=64)
+            for part, first in ((0, RE), (1, IM)):
+                nc.vector.tensor_copy(
+                    out=grouped[:, first : first + POSITIONS, :].rearrange("p (b q) j -> p b q j", b=BATCH),
+                    in_=x_raw[n][:, :, :, :, part].rearrange("p b j q -> p b q j"),
+                )
+            nc.vector.tensor_scalar_mul(
+                out=grouped[:, NEG : NEG + POSITIONS, :], in0=grouped[:, IM : IM + POSITIONS, :], scalar1=-1.0
+            )
+            codes = stage.tile([P, SETS], U32, name="x_codes", align_bytes=64)
+            scales = stage.tile([P, SETS], U8, name="x_scales", align_bytes=64)
+            quantise_sets(nc, grouped, codes, scales)
+            x_mx[n] = (codes, scales)
+
+        def prepare_weights(layer, n):
+            codes = weights.tile([P, PARTS, WIDTH], U32, name="w_codes%d_%d" % (layer, n), align_bytes=64)
+            scales = weights.tile([P, PARTS, WIDTH], U8, name="w_scales%d_%d" % (layer, n), align_bytes=64)
+            for part in range(PARTS):
+                grouped = w_stage.tile([P, WIDTH, PACK], BF16, name="w_grouped", align_bytes=64)
+                grouped_view = grouped[:].rearrange("p (c i) j -> p c j i", i=4)
+                raw_view = w_raw[(layer, n, part)][:].rearrange("p j (c i) -> p c j i", i=4)
+                if n == 0 and part == 1:
+                    nc.vector.tensor_copy(out=grouped_view, in_=raw_view)
+                else:
+                    nc.scalar.copy(out=grouped_view, in_=raw_view)
+                nc.vector.quantize_mx(
+                    out=codes[:, part, :].bitcast(FP8X4),
+                    scales=scales[:, part, :],
+                    in_=grouped[:].rearrange("p c j -> p (c j)"),
+                )
+            w_mx[(layer, n)] = (codes, scales)
+
+        def layer1(n):
+            planes[n] = stage.tile([P, PARTS, TILES, POSITIONS], BF16, name="planes")
+            for t in range(TILES):
+                for part in range(PARTS):
+                    hidden = psum_hidden.tile([P, POSITIONS], F32, name="hidden", tag="hidden")
+                    for first, count in POSITION_RANGES:
+                        complex_product(
+                            nc, hidden[:, first : first + count], w_mx[(1, n)][0], w_mx[(1, n)][1], t,
+                            x_mx[n][0], x_mx[n][1], part, first, count,
+                        )
+                    nc.scalar.activation(
+                        out=planes[n][:, part, t, :], in_=hidden[:], func=RELU,
+                        bias=bias1[:, part, n, t : t + 1], scale=1.0,
+                    )
+
+        def prepare_hidden(n):
+            grouped = stage.tile([P, SETS, PACK], BF16, name="h_grouped", align_bytes=64)
+            for part, first in ((0, RE), (1, IM)):
+                nc.vector.tensor_copy(
+                    out=grouped[:, first : first + POSITIONS, :].rearrange("p (c i) t -> p c t i", i=4),
+                    in_=planes[n][:, part, :, :].rearrange("p t (c i) -> p c t i", i=4),
+                )
+            nc.vector.tensor_scalar_mul(
+                out=grouped[:, NEG : NEG + POSITIONS, :], in0=grouped[:, IM : IM + POSITIONS, :], scalar1=-1.0
+            )
+            codes = stage.tile([P, SETS], U32, name="h_codes", align_bytes=64)
+            scales = stage.tile([P, SETS], U8, name="h_scales", align_bytes=64)
+            quantise_sets(nc, grouped, codes, scales)
+            h_mx[n] = (codes, scales)
+
+        def layer2(n):
+            for t in range(TILES):
+                result = results.tile([P, POSITIONS, PARTS], F32, name="result")
+                for first, count in POSITION_RANGES:
+                    pair = psum_out.tile([P, PARTS, count], F32, name="pair", tag="pair")
+                    for part in range(PARTS):
+                        complex_product(
+                            nc, pair[:, part, :], w_mx[(2, n)][0], w_mx[(2, n)][1], t,
+                            h_mx[n][0], h_mx[n][1], part, first, count,
+                        )
+                    nc.vector.tensor_tensor(
+                        out=result[:, first : first + count, :],
+                        in0=pair[:].rearrange("p r q -> p q r"),
+                        in1=bias2[:, n, t, :].unsqueeze(1).to_broadcast([P, count, PARTS]),
+                        op=ADD,
+                    )
+                nc.sync.dma_start(out=out_view[n, t], in_=result[:].rearrange("p (b q) r -> p b (q r)", b=BATCH))
+
+        bias_rows = const.tile([P, P], BF16)
+        nc.gpsimd.memset(bias_rows[:], 0.0)
+        rows = PARTS * BLOCKS * TILES
+        nc.sync.dma_start(out=bias_rows[0:rows, :], in_=b1.rearrange("r n (t c) -> (r n t) c", c=P))
+        nc.sync.dma_start(out=bias_rows[rows : 2 * rows, :], in_=b2.rearrange("r n (t c) -> (r n t) c", c=P))
+        load_x(0)
+        load_weights(1, 0)
+        for n in range(-1, BLOCKS):
+            if n + 2 < BLOCKS:
+                load_x(n + 2)
+                load_weights(1, n + 2)
+            if n + 1 < BLOCKS:
+                load_weights(2, n + 1)
+
+        identity = const.tile([P, P], BF16)
+        make_identity(nc, identity[:])
+        bias_t = psum_hidden.tile([P, P], BF16, name="bias_t", tag="hidden")
+        nc.tensor.transpose(out=bias_t[:], in_=bias_rows[:], identity=identity[:])
+        bias1 = const.tile([P, PARTS, BLOCKS, TILES], F32)
+        nc.vector.tensor_copy(out=bias1[:].rearrange("p r n t -> p (r n t)"), in_=bias_t[:, 0:rows])
+        bias2 = const.tile([P, BLOCKS, TILES, PARTS], F32)
+        nc.vector.tensor_copy(
+            out=bias2[:].rearrange("p n t r -> p (n t) r"),
+            in_=bias_t[:, rows : 2 * rows].rearrange("p (r c) -> p c r", r=PARTS),
+        )
+
+        prepare_x(0)
+        prepare_weights(1, 0)
+        for n in range(-1, BLOCKS):
+            if n + 1 < BLOCKS:
+                layer1(n + 1)
+            if n >= 0:
+                prepare_hidden(n)
+            if n + 2 < BLOCKS:
+                prepare_x(n + 2)
+            if n >= 0:
+                layer2(n)
+            if n + 2 < BLOCKS:
+                prepare_weights(1, n + 2)
+            if n + 1 < BLOCKS:
+                prepare_weights(2, n + 1)

@@ -92,8 +92,8 @@ def tile_scatteringmodule_pa_kernel(tc, xh, w1, w2, b1, b2, out):
             grouped = stage.tile([P, SETS, PACK], BF16, name="x_grouped", align_bytes=64)
             for part, first in ((0, RE), (1, IM)):
                 nc.vector.tensor_copy(
-                    out=grouped[:, first : first + POSITIONS, :].rearrange("p (b q) j -> p b q j", b=BATCH),
-                    in_=x_raw[n][:, :, :, :, part].rearrange("p b j q -> p b q j"),
+                    out=grouped[:, first : first + POSITIONS, :].rearrange("p (b c i) j -> p b c j i", b=BATCH, i=4),
+                    in_=x_raw[n][:, :, :, :, part].rearrange("p b j (c i) -> p b c j i", i=4),
                 )
             nc.vector.tensor_scalar_mul(
                 out=grouped[:, NEG : NEG + POSITIONS, :], in0=grouped[:, IM : IM + POSITIONS, :], scalar1=-1.0
@@ -123,8 +123,8 @@ def tile_scatteringmodule_pa_kernel(tc, xh, w1, w2, b1, b2, out):
 
         def layer1(n):
             planes[n] = stage.tile([P, PARTS, TILES, POSITIONS], BF16, name="planes")
-            for t in range(TILES):
-                for part in range(PARTS):
+            for part in range(PARTS):
+                for t in range(TILES):
                     hidden = psum_hidden.tile([P, POSITIONS], F32, name="hidden", tag="hidden")
                     for first, count in POSITION_RANGES:
                         complex_product(

@@ -60,6 +60,8 @@ def tile_scatteringmodule_pa_kernel(tc, xh, w1, w2, b1, b2, out):
     with (
         tc.tile_pool(name="const", bufs=1) as const,
         tc.tile_pool(name="raw", bufs=1) as raw,
+        tc.tile_pool(name="w_raw_pool", bufs=12) as w_raw_pool,
+        tc.tile_pool(name="hidden_mx", bufs=1) as hidden_mx,
         tc.tile_pool(name="weights", bufs=1) as weights,
         tc.tile_pool(name="stage", bufs=2) as stage,
         tc.tile_pool(name="w_stage", bufs=3) as w_stage,
@@ -80,7 +82,7 @@ def tile_scatteringmodule_pa_kernel(tc, xh, w1, w2, b1, b2, out):
 
         def load_weights(layer, n):
             for part in range(PARTS):
-                w_tile = raw.tile([P, PACK, WIDTH], BF16, name="w_raw%d_%d_%d" % (layer, n, part))
+                w_tile = w_raw_pool.tile([P, PACK, WIDTH], BF16, name="w_raw")
                 if layer == 1:
                     source = w1[part, n].rearrange("(p j) k -> p j k", j=PACK)
                 else:
@@ -90,8 +92,8 @@ def tile_scatteringmodule_pa_kernel(tc, xh, w1, w2, b1, b2, out):
 
         def prepare_x(n):
             grouped = stage.tile([P, SETS, PACK], BF16, name="x_grouped", align_bytes=64)
-            for part, first in ((0, RE), (1, IM)):
-                nc.vector.tensor_copy(
+            for part, first, copy in ((0, RE, nc.scalar.copy), (1, IM, nc.vector.tensor_copy)):
+                copy(
                     out=grouped[:, first : first + POSITIONS, :].rearrange("p (b c i) j -> p b c j i", b=BATCH, i=4),
                     in_=x_raw[n][:, :, :, :, part].rearrange("p b j (c i) -> p b c j i", i=4),
                 )
@@ -110,7 +112,7 @@ def tile_scatteringmodule_pa_kernel(tc, xh, w1, w2, b1, b2, out):
                 grouped = w_stage.tile([P, WIDTH, PACK], BF16, name="w_grouped", align_bytes=64)
                 grouped_view = grouped[:].rearrange("p (c i) j -> p c j i", i=4)
                 raw_view = w_raw[(layer, n, part)][:].rearrange("p j (c i) -> p c j i", i=4)
-                if n == 0 and part == 1:
+                if layer == 1 and part == 1:
                     nc.vector.tensor_copy(out=grouped_view, in_=raw_view)
                 else:
                     nc.scalar.copy(out=grouped_view, in_=raw_view)
@@ -146,8 +148,8 @@ def tile_scatteringmodule_pa_kernel(tc, xh, w1, w2, b1, b2, out):
             nc.vector.tensor_scalar_mul(
                 out=grouped[:, NEG : NEG + POSITIONS, :], in0=grouped[:, IM : IM + POSITIONS, :], scalar1=-1.0
             )
-            codes = stage.tile([P, SETS], U32, name="h_codes", align_bytes=64)
-            scales = stage.tile([P, SETS], U8, name="h_scales", align_bytes=64)
+            codes = hidden_mx.tile([P, SETS], U32, name="h_codes%d" % n, align_bytes=64)
+            scales = hidden_mx.tile([P, SETS], U8, name="h_scales%d" % n, align_bytes=64)
             quantise_sets(nc, grouped, codes, scales)
             h_mx[n] = (codes, scales)
 
@@ -174,14 +176,11 @@ def tile_scatteringmodule_pa_kernel(tc, xh, w1, w2, b1, b2, out):
         rows = PARTS * BLOCKS * TILES
         nc.sync.dma_start(out=bias_rows[0:rows, :], in_=b1.rearrange("r n (t c) -> (r n t) c", c=P))
         nc.sync.dma_start(out=bias_rows[rows : 2 * rows, :], in_=b2.rearrange("r n (t c) -> (r n t) c", c=P))
-        load_x(0)
-        load_weights(1, 0)
-        for n in range(-1, BLOCKS):
-            if n + 2 < BLOCKS:
-                load_x(n + 2)
-                load_weights(1, n + 2)
-            if n + 1 < BLOCKS:
-                load_weights(2, n + 1)
+        for n in range(BLOCKS):
+            load_x(n)
+            load_weights(1, n)
+        for n in range(BLOCKS):
+            load_weights(2, n)
 
         identity = const.tile([P, P], BF16)
         make_identity(nc, identity[:])
@@ -197,16 +196,14 @@ def tile_scatteringmodule_pa_kernel(tc, xh, w1, w2, b1, b2, out):
 
         prepare_x(0)
         prepare_weights(1, 0)
-        for n in range(-1, BLOCKS):
+        for n in range(BLOCKS):
+            layer1(n)
             if n + 1 < BLOCKS:
-                layer1(n + 1)
-            if n >= 0:
-                prepare_hidden(n)
-            if n + 2 < BLOCKS:
-                prepare_x(n + 2)
-            if n >= 0:
-                layer2(n)
-            if n + 2 < BLOCKS:
-                prepare_weights(1, n + 2)
+                prepare_x(n + 1)
+                prepare_weights(1, n + 1)
+            prepare_hidden(n)
+        prepare_weights(2, 0)
+        for n in range(BLOCKS):
             if n + 1 < BLOCKS:
                 prepare_weights(2, n + 1)
+            layer2(n)

@@ -13,6 +13,7 @@ ADD = mybir.AluOpType.add
 
 P = 128
 PACK = 4
+RUN = 4
 BATCH = 4
 BLOCKS = 4
 WIDTH = 512
@@ -20,12 +21,13 @@ TILES = WIDTH // P
 SPOTS = 96
 POSITIONS = BATCH * SPOTS
 PARTS = 2
+REAL, IMAG = 0, 1
 
-NEG, RE, IM = 0, POSITIONS, 2 * POSITIONS
+RE, IM, NEG = 0, POSITIONS, 2 * POSITIONS
 SETS = 3 * POSITIONS
 MOVING = ((RE, NEG), (IM, RE))
 POSITION_RANGES = ((0, 256), (256, 128))
-QUANTISE_RANGES = ((0, 1024), (1024, 128))
+QUANTISE_RANGES = ((0, 512), (512, 512), (1024, 128))
 
 
 def quantise_sets(nc, grouped, codes, scales):
@@ -37,7 +39,15 @@ def quantise_sets(nc, grouped, codes, scales):
         )
 
 
-def complex_product(nc, acc, w_codes, w_scales, tile_index, a_codes, a_scales, part, first, count):
+def negate_imaginary(nc, grouped):
+    nc.vector.tensor_scalar_mul(
+        out=grouped[:, NEG : NEG + POSITIONS, :], in0=grouped[:, IM : IM + POSITIONS, :], scalar1=-1.0
+    )
+
+
+def complex_product(nc, acc, weight, tile_index, activation, part, first, count):
+    w_codes, w_scales = weight
+    a_codes, a_scales = activation
     columns = slice(tile_index * P, (tile_index + 1) * P)
     for w_part in range(PARTS):
         start = MOVING[part][w_part] + first
@@ -59,10 +69,10 @@ def tile_scatteringmodule_pa_kernel(tc, xh, w1, w2, b1, b2, out):
 
     with (
         tc.tile_pool(name="const", bufs=1) as const,
-        tc.tile_pool(name="raw", bufs=1) as raw,
+        tc.tile_pool(name="x_raw_pool", bufs=1) as x_raw_pool,
         tc.tile_pool(name="w_raw_pool", bufs=12) as w_raw_pool,
-        tc.tile_pool(name="hidden_mx", bufs=1) as hidden_mx,
         tc.tile_pool(name="weights", bufs=1) as weights,
+        tc.tile_pool(name="hidden_mx", bufs=1) as hidden_mx,
         tc.tile_pool(name="stage", bufs=2) as stage,
         tc.tile_pool(name="w_stage", bufs=3) as w_stage,
         tc.tile_pool(name="results", bufs=4) as results,
@@ -77,7 +87,7 @@ def tile_scatteringmodule_pa_kernel(tc, xh, w1, w2, b1, b2, out):
         h_mx = {}
 
         def load_x(n):
-            x_raw[n] = raw.tile([P, BATCH, PACK, SPOTS, PARTS], BF16, name="x_raw%d" % n)
+            x_raw[n] = x_raw_pool.tile([P, BATCH, PACK, SPOTS, PARTS], BF16, name="x_raw%d" % n)
             nc.sync.dma_start(out=x_raw[n][:].rearrange("p b j q r -> p b (j q r)"), in_=x_view[n])
 
         def load_weights(layer, n):
@@ -90,48 +100,54 @@ def tile_scatteringmodule_pa_kernel(tc, xh, w1, w2, b1, b2, out):
                 nc.sync.dma_start(out=w_tile[:], in_=source)
                 w_raw[(layer, n, part)] = w_tile
 
-        def prepare_x(n):
-            grouped = stage.tile([P, SETS, PACK], BF16, name="x_grouped", align_bytes=64)
-            for part, first, copy in ((0, RE, nc.scalar.copy), (1, IM, nc.vector.tensor_copy)):
+        def regroup_weights(layer, n):
+            grouped = []
+            for part in range(PARTS):
+                tile = w_stage.tile([P, WIDTH, PACK], BF16, name="w_grouped", align_bytes=64)
+                copy = nc.vector.tensor_copy if (layer == 1 and part == IMAG) else nc.scalar.copy
                 copy(
-                    out=grouped[:, first : first + POSITIONS, :].rearrange("p (b c i) j -> p b c j i", b=BATCH, i=4),
-                    in_=x_raw[n][:, :, :, :, part].rearrange("p b j (c i) -> p b c j i", i=4),
+                    out=tile[:].rearrange("p (c i) j -> p c j i", i=RUN),
+                    in_=w_raw[(layer, n, part)][:].rearrange("p j (c i) -> p c j i", i=RUN),
                 )
-            nc.vector.tensor_scalar_mul(
-                out=grouped[:, NEG : NEG + POSITIONS, :], in0=grouped[:, IM : IM + POSITIONS, :], scalar1=-1.0
-            )
-            codes = stage.tile([P, SETS], U32, name="x_codes", align_bytes=64)
-            scales = stage.tile([P, SETS], U8, name="x_scales", align_bytes=64)
-            quantise_sets(nc, grouped, codes, scales)
-            x_mx[n] = (codes, scales)
+                grouped.append(tile)
+            return grouped
 
-        def prepare_weights(layer, n):
+        def quantise_weights(layer, n, grouped):
             codes = weights.tile([P, PARTS, WIDTH], U32, name="w_codes%d_%d" % (layer, n), align_bytes=64)
             scales = weights.tile([P, PARTS, WIDTH], U8, name="w_scales%d_%d" % (layer, n), align_bytes=64)
             for part in range(PARTS):
-                grouped = w_stage.tile([P, WIDTH, PACK], BF16, name="w_grouped", align_bytes=64)
-                grouped_view = grouped[:].rearrange("p (c i) j -> p c j i", i=4)
-                raw_view = w_raw[(layer, n, part)][:].rearrange("p j (c i) -> p c j i", i=4)
-                if layer == 1 and part == 1:
-                    nc.vector.tensor_copy(out=grouped_view, in_=raw_view)
-                else:
-                    nc.scalar.copy(out=grouped_view, in_=raw_view)
                 nc.vector.quantize_mx(
                     out=codes[:, part, :].bitcast(FP8X4),
                     scales=scales[:, part, :],
-                    in_=grouped[:].rearrange("p c j -> p (c j)"),
+                    in_=grouped[part][:].rearrange("p c j -> p (c j)"),
                 )
             w_mx[(layer, n)] = (codes, scales)
 
+        def prepare_layer1(n):
+            x_grouped = stage.tile([P, SETS, PACK], BF16, name="x_grouped", align_bytes=64)
+            for part, first, copy in ((REAL, RE, nc.scalar.copy), (IMAG, IM, nc.vector.tensor_copy)):
+                copy(
+                    out=x_grouped[:, first : first + POSITIONS, :].rearrange(
+                        "p (b c i) j -> p b c j i", b=BATCH, i=RUN
+                    ),
+                    in_=x_raw[n][:, :, :, :, part].rearrange("p b j (c i) -> p b c j i", i=RUN),
+                )
+            w_grouped = regroup_weights(1, n)
+            negate_imaginary(nc, x_grouped)
+            codes = stage.tile([P, SETS], U32, name="x_codes", align_bytes=64)
+            scales = stage.tile([P, SETS], U8, name="x_scales", align_bytes=64)
+            quantise_sets(nc, x_grouped, codes, scales)
+            x_mx[n] = (codes, scales)
+            quantise_weights(1, n, w_grouped)
+
         def layer1(n):
             planes[n] = stage.tile([P, PARTS, TILES, POSITIONS], BF16, name="planes")
-            for part in range(PARTS):
+            for part in (IMAG, REAL):
                 for t in range(TILES):
                     hidden = psum_hidden.tile([P, POSITIONS], F32, name="hidden", tag="hidden")
                     for first, count in POSITION_RANGES:
                         complex_product(
-                            nc, hidden[:, first : first + count], w_mx[(1, n)][0], w_mx[(1, n)][1], t,
-                            x_mx[n][0], x_mx[n][1], part, first, count,
+                            nc, hidden[:, first : first + count], w_mx[(1, n)], t, x_mx[n], part, first, count
                         )
                     nc.scalar.activation(
                         out=planes[n][:, part, t, :], in_=hidden[:], func=RELU,
@@ -140,14 +156,12 @@ def tile_scatteringmodule_pa_kernel(tc, xh, w1, w2, b1, b2, out):
 
         def prepare_hidden(n):
             grouped = stage.tile([P, SETS, PACK], BF16, name="h_grouped", align_bytes=64)
-            for part, first in ((0, RE), (1, IM)):
+            for part, first in ((IMAG, IM), (REAL, RE)):
                 nc.vector.tensor_copy(
-                    out=grouped[:, first : first + POSITIONS, :].rearrange("p (c i) t -> p c t i", i=4),
-                    in_=planes[n][:, part, :, :].rearrange("p t (c i) -> p c t i", i=4),
+                    out=grouped[:, first : first + POSITIONS, :].rearrange("p (c i) t -> p c t i", i=RUN),
+                    in_=planes[n][:, part, :, :].rearrange("p t (c i) -> p c t i", i=RUN),
                 )
-            nc.vector.tensor_scalar_mul(
-                out=grouped[:, NEG : NEG + POSITIONS, :], in0=grouped[:, IM : IM + POSITIONS, :], scalar1=-1.0
-            )
+            negate_imaginary(nc, grouped)
             codes = hidden_mx.tile([P, SETS], U32, name="h_codes%d" % n, align_bytes=64)
             scales = hidden_mx.tile([P, SETS], U8, name="h_scales%d" % n, align_bytes=64)
             quantise_sets(nc, grouped, codes, scales)
@@ -159,10 +173,7 @@ def tile_scatteringmodule_pa_kernel(tc, xh, w1, w2, b1, b2, out):
                 for first, count in POSITION_RANGES:
                     pair = psum_out.tile([P, PARTS, count], F32, name="pair", tag="pair")
                     for part in range(PARTS):
-                        complex_product(
-                            nc, pair[:, part, :], w_mx[(2, n)][0], w_mx[(2, n)][1], t,
-                            h_mx[n][0], h_mx[n][1], part, first, count,
-                        )
+                        complex_product(nc, pair[:, part, :], w_mx[(2, n)], t, h_mx[n], part, first, count)
                     nc.vector.tensor_tensor(
                         out=result[:, first : first + count, :],
                         in0=pair[:].rearrange("p r q -> p q r"),
@@ -171,12 +182,14 @@ def tile_scatteringmodule_pa_kernel(tc, xh, w1, w2, b1, b2, out):
                     )
                 nc.sync.dma_start(out=out_view[n, t], in_=result[:].rearrange("p (b q) r -> p b (q r)", b=BATCH))
 
+        load_x(0)
+        load_weights(1, 0)
         bias_rows = const.tile([P, P], BF16)
         nc.gpsimd.memset(bias_rows[:], 0.0)
         rows = PARTS * BLOCKS * TILES
         nc.sync.dma_start(out=bias_rows[0:rows, :], in_=b1.rearrange("r n (t c) -> (r n t) c", c=P))
         nc.sync.dma_start(out=bias_rows[rows : 2 * rows, :], in_=b2.rearrange("r n (t c) -> (r n t) c", c=P))
-        for n in range(BLOCKS):
+        for n in range(1, BLOCKS):
             load_x(n)
             load_weights(1, n)
         for n in range(BLOCKS):
@@ -194,16 +207,14 @@ def tile_scatteringmodule_pa_kernel(tc, xh, w1, w2, b1, b2, out):
             in_=bias_t[:, rows : 2 * rows].rearrange("p (r c) -> p c r", r=PARTS),
         )
 
-        prepare_x(0)
-        prepare_weights(1, 0)
+        prepare_layer1(0)
         for n in range(BLOCKS):
             layer1(n)
             if n + 1 < BLOCKS:
-                prepare_x(n + 1)
-                prepare_weights(1, n + 1)
+                prepare_layer1(n + 1)
             prepare_hidden(n)
-        prepare_weights(2, 0)
+        quantise_weights(2, 0, regroup_weights(2, 0))
         for n in range(BLOCKS):
             if n + 1 < BLOCKS:
-                prepare_weights(2, n + 1)
+                quantise_weights(2, n + 1, regroup_weights(2, n + 1))
             layer2(n)

@@ -22,15 +22,19 @@ SPOTS = 96
 POSITIONS = BATCH * SPOTS
 PARTS = 2
 REAL, IMAG = 0, 1
+BIAS_ROWS = PARTS * BLOCKS * TILES
 
-RE, IM, NEG = 0, POSITIONS, 2 * POSITIONS
+NEG, RE, IM = 0, POSITIONS, 2 * POSITIONS
 SETS = 3 * POSITIONS
 MOVING = ((RE, NEG), (IM, RE))
 POSITION_RANGES = ((0, 256), (256, 128))
-QUANTISE_RANGES = ((0, 512), (512, 512), (1024, 128))
+QUANTISE_RANGES = ((0, 1024), (1024, 128))
 
 
-def quantise_sets(nc, grouped, codes, scales):
+def negate_and_quantise(nc, grouped, codes, scales):
+    nc.vector.tensor_scalar_mul(
+        out=grouped[:, NEG : NEG + POSITIONS, :], in0=grouped[:, IM : IM + POSITIONS, :], scalar1=-1.0
+    )
     for first, count in QUANTISE_RANGES:
         nc.vector.quantize_mx(
             out=codes[:, first : first + count].bitcast(FP8X4),
@@ -39,22 +43,16 @@ def quantise_sets(nc, grouped, codes, scales):
         )
 
 
-def negate_imaginary(nc, grouped):
-    nc.vector.tensor_scalar_mul(
-        out=grouped[:, NEG : NEG + POSITIONS, :], in0=grouped[:, IM : IM + POSITIONS, :], scalar1=-1.0
-    )
-
-
-def complex_product(nc, acc, weight, tile_index, activation, part, first, count):
+def complex_product(nc, acc, weight, t, activation, part, first, count):
     w_codes, w_scales = weight
     a_codes, a_scales = activation
-    columns = slice(tile_index * P, (tile_index + 1) * P)
+    channels = slice(t * P, (t + 1) * P)
     for w_part in range(PARTS):
         start = MOVING[part][w_part] + first
         nc.tensor.matmul_mx(
             out=acc,
-            lhsT=w_codes[:, w_part, columns].bitcast(FP8X4),
-            lhsT_scale=w_scales[:, w_part, columns],
+            lhsT=w_codes[:, w_part, channels].bitcast(FP8X4),
+            lhsT_scale=w_scales[:, w_part, channels],
             rhs=a_codes[:, start : start + count].bitcast(FP8X4),
             rhs_scale=a_scales[:, start : start + count],
             start=(w_part == 0),
@@ -69,15 +67,14 @@ def tile_scatteringmodule_pa_kernel(tc, xh, w1, w2, b1, b2, out):
 
     with (
         tc.tile_pool(name="const", bufs=1) as const,
-        tc.tile_pool(name="x_raw_pool", bufs=1) as x_raw_pool,
+        tc.tile_pool(name="raw", bufs=1) as raw,
         tc.tile_pool(name="w_raw_pool", bufs=12) as w_raw_pool,
-        tc.tile_pool(name="weights", bufs=1) as weights,
         tc.tile_pool(name="hidden_mx", bufs=1) as hidden_mx,
+        tc.tile_pool(name="weights", bufs=1) as weights,
         tc.tile_pool(name="stage", bufs=2) as stage,
         tc.tile_pool(name="w_stage", bufs=3) as w_stage,
-        tc.tile_pool(name="results", bufs=4) as results,
-        tc.psum_pool(name="psum_hidden", bufs=4) as psum_hidden,
-        tc.psum_pool(name="psum_out", bufs=4) as psum_out,
+        tc.tile_pool(name="results", bufs=6) as results,
+        tc.psum_pool(name="psum", bufs=8) as psum,
     ):
         x_raw = {}
         w_raw = {}
@@ -87,68 +84,55 @@ def tile_scatteringmodule_pa_kernel(tc, xh, w1, w2, b1, b2, out):
         h_mx = {}
 
         def load_x(n):
-            x_raw[n] = x_raw_pool.tile([P, BATCH, PACK, SPOTS, PARTS], BF16, name="x_raw%d" % n)
+            x_raw[n] = raw.tile([P, BATCH, PACK, SPOTS, PARTS], BF16, name="x_raw%d" % n)
             nc.sync.dma_start(out=x_raw[n][:].rearrange("p b j q r -> p b (j q r)"), in_=x_view[n])
 
         def load_weights(layer, n):
             for part in range(PARTS):
                 w_tile = w_raw_pool.tile([P, PACK, WIDTH], BF16, name="w_raw")
                 if layer == 1:
-                    source = w1[part, n].rearrange("(p j) k -> p j k", j=PACK)
+                    rows = w1[part, n].rearrange("(p j) k -> p j k", j=PACK)
                 else:
-                    source = w2[part, n].rearrange("(t p) k -> p t k", p=P)
-                nc.sync.dma_start(out=w_tile[:], in_=source)
+                    rows = w2[part, n].rearrange("(t p) k -> p t k", p=P)
+                nc.sync.dma_start(out=w_tile[:], in_=rows)
                 w_raw[(layer, n, part)] = w_tile
 
-        def regroup_weights(layer, n):
-            grouped = []
-            for part in range(PARTS):
-                tile = w_stage.tile([P, WIDTH, PACK], BF16, name="w_grouped", align_bytes=64)
-                copy = nc.vector.tensor_copy if (layer == 1 and part == IMAG) else nc.scalar.copy
+        def prepare_x(n):
+            grouped = stage.tile([P, SETS, PACK], BF16, name="x_grouped", align_bytes=64)
+            for part, first, copy in ((REAL, RE, nc.scalar.copy), (IMAG, IM, nc.vector.tensor_copy)):
                 copy(
-                    out=tile[:].rearrange("p (c i) j -> p c j i", i=RUN),
-                    in_=w_raw[(layer, n, part)][:].rearrange("p j (c i) -> p c j i", i=RUN),
+                    out=grouped[:, first : first + POSITIONS, :].rearrange("p (b c i) j -> p b c j i", b=BATCH, i=RUN),
+                    in_=x_raw[n][:, :, :, :, part].rearrange("p b j (c i) -> p b c j i", i=RUN),
                 )
-                grouped.append(tile)
-            return grouped
+            codes = stage.tile([P, SETS], U32, name="x_codes", align_bytes=64)
+            scales = stage.tile([P, SETS], U8, name="x_scales", align_bytes=64)
+            negate_and_quantise(nc, grouped, codes, scales)
+            x_mx[n] = (codes, scales)
 
-        def quantise_weights(layer, n, grouped):
+        def prepare_weights(layer, n):
             codes = weights.tile([P, PARTS, WIDTH], U32, name="w_codes%d_%d" % (layer, n), align_bytes=64)
             scales = weights.tile([P, PARTS, WIDTH], U8, name="w_scales%d_%d" % (layer, n), align_bytes=64)
             for part in range(PARTS):
+                grouped = w_stage.tile([P, WIDTH, PACK], BF16, name="w_grouped", align_bytes=64)
+                copy = nc.vector.tensor_copy if (layer == 1 and part == IMAG) else nc.scalar.copy
+                copy(
+                    out=grouped[:].rearrange("p (c i) j -> p c j i", i=RUN),
+                    in_=w_raw[(layer, n, part)][:].rearrange("p j (c i) -> p c j i", i=RUN),
+                )
                 nc.vector.quantize_mx(
                     out=codes[:, part, :].bitcast(FP8X4),
                     scales=scales[:, part, :],
-                    in_=grouped[part][:].rearrange("p c j -> p (c j)"),
+                    in_=grouped[:].rearrange("p c j -> p (c j)"),
                 )
             w_mx[(layer, n)] = (codes, scales)
 
-        def prepare_layer1(n):
-            x_grouped = stage.tile([P, SETS, PACK], BF16, name="x_grouped", align_bytes=64)
-            for part, first, copy in ((REAL, RE, nc.scalar.copy), (IMAG, IM, nc.vector.tensor_copy)):
-                copy(
-                    out=x_grouped[:, first : first + POSITIONS, :].rearrange(
-                        "p (b c i) j -> p b c j i", b=BATCH, i=RUN
-                    ),
-                    in_=x_raw[n][:, :, :, :, part].rearrange("p b j (c i) -> p b c j i", i=RUN),
-                )
-            w_grouped = regroup_weights(1, n)
-            negate_imaginary(nc, x_grouped)
-            codes = stage.tile([P, SETS], U32, name="x_codes", align_bytes=64)
-            scales = stage.tile([P, SETS], U8, name="x_scales", align_bytes=64)
-            quantise_sets(nc, x_grouped, codes, scales)
-            x_mx[n] = (codes, scales)
-            quantise_weights(1, n, w_grouped)
-
         def layer1(n):
             planes[n] = stage.tile([P, PARTS, TILES, POSITIONS], BF16, name="planes")
-            for part in (IMAG, REAL):
+            for part in range(PARTS):
                 for t in range(TILES):
-                    hidden = psum_hidden.tile([P, POSITIONS], F32, name="hidden", tag="hidden")
+                    hidden = psum.tile([P, POSITIONS], F32, name="hidden", tag="bank")
                     for first, count in POSITION_RANGES:
-                        complex_product(
-                            nc, hidden[:, first : first + count], w_mx[(1, n)], t, x_mx[n], part, first, count
-                        )
+                        complex_product(nc, hidden[:, first : first + count], w_mx[(1, n)], t, x_mx[n], part, first, count)
                     nc.scalar.activation(
                         out=planes[n][:, part, t, :], in_=hidden[:], func=RELU,
                         bias=bias1[:, part, n, t : t + 1], scale=1.0,
@@ -156,22 +140,21 @@ def tile_scatteringmodule_pa_kernel(tc, xh, w1, w2, b1, b2, out):
 
         def prepare_hidden(n):
             grouped = stage.tile([P, SETS, PACK], BF16, name="h_grouped", align_bytes=64)
-            for part, first in ((IMAG, IM), (REAL, RE)):
+            for part, first in ((REAL, RE), (IMAG, IM)):
                 nc.vector.tensor_copy(
                     out=grouped[:, first : first + POSITIONS, :].rearrange("p (c i) t -> p c t i", i=RUN),
                     in_=planes[n][:, part, :, :].rearrange("p t (c i) -> p c t i", i=RUN),
                 )
-            negate_imaginary(nc, grouped)
             codes = hidden_mx.tile([P, SETS], U32, name="h_codes%d" % n, align_bytes=64)
             scales = hidden_mx.tile([P, SETS], U8, name="h_scales%d" % n, align_bytes=64)
-            quantise_sets(nc, grouped, codes, scales)
+            negate_and_quantise(nc, grouped, codes, scales)
             h_mx[n] = (codes, scales)
 
         def layer2(n):
             for t in range(TILES):
                 result = results.tile([P, POSITIONS, PARTS], F32, name="result")
                 for first, count in POSITION_RANGES:
-                    pair = psum_out.tile([P, PARTS, count], F32, name="pair", tag="pair")
+                    pair = psum.tile([P, PARTS, count], F32, name="pair", tag="bank")
                     for part in range(PARTS):
                         complex_product(nc, pair[:, part, :], w_mx[(2, n)], t, h_mx[n], part, first, count)
                     nc.vector.tensor_tensor(
@@ -182,14 +165,11 @@ def tile_scatteringmodule_pa_kernel(tc, xh, w1, w2, b1, b2, out):
                     )
                 nc.sync.dma_start(out=out_view[n, t], in_=result[:].rearrange("p (b q) r -> p b (q r)", b=BATCH))
 
-        load_x(0)
-        load_weights(1, 0)
         bias_rows = const.tile([P, P], BF16)
         nc.gpsimd.memset(bias_rows[:], 0.0)
-        rows = PARTS * BLOCKS * TILES
-        nc.sync.dma_start(out=bias_rows[0:rows, :], in_=b1.rearrange("r n (t c) -> (r n t) c", c=P))
-        nc.sync.dma_start(out=bias_rows[rows : 2 * rows, :], in_=b2.rearrange("r n (t c) -> (r n t) c", c=P))
-        for n in range(1, BLOCKS):
+        nc.sync.dma_start(out=bias_rows[0:BIAS_ROWS, :], in_=b1.rearrange("r n (t c) -> (r n t) c", c=P))
+        nc.sync.dma_start(out=bias_rows[BIAS_ROWS : 2 * BIAS_ROWS, :], in_=b2.rearrange("r n (t c) -> (r n t) c", c=P))
+        for n in range(BLOCKS):
             load_x(n)
             load_weights(1, n)
         for n in range(BLOCKS):
@@ -197,24 +177,26 @@ def tile_scatteringmodule_pa_kernel(tc, xh, w1, w2, b1, b2, out):
 
         identity = const.tile([P, P], BF16)
         make_identity(nc, identity[:])
-        bias_t = psum_hidden.tile([P, P], BF16, name="bias_t", tag="hidden")
+        bias_t = psum.tile([P, P], BF16, name="bias_t", tag="bank")
         nc.tensor.transpose(out=bias_t[:], in_=bias_rows[:], identity=identity[:])
         bias1 = const.tile([P, PARTS, BLOCKS, TILES], F32)
-        nc.vector.tensor_copy(out=bias1[:].rearrange("p r n t -> p (r n t)"), in_=bias_t[:, 0:rows])
+        nc.vector.tensor_copy(out=bias1[:].rearrange("p r n t -> p (r n t)"), in_=bias_t[:, 0:BIAS_ROWS])
         bias2 = const.tile([P, BLOCKS, TILES, PARTS], F32)
         nc.vector.tensor_copy(
             out=bias2[:].rearrange("p n t r -> p (n t) r"),
-            in_=bias_t[:, rows : 2 * rows].rearrange("p (r c) -> p c r", r=PARTS),
+            in_=bias_t[:, BIAS_ROWS : 2 * BIAS_ROWS].rearrange("p (r c) -> p c r", r=PARTS),
         )
 
-        prepare_layer1(0)
+        prepare_x(0)
+        prepare_weights(1, 0)
         for n in range(BLOCKS):
             layer1(n)
             if n + 1 < BLOCKS:
-                prepare_layer1(n + 1)
+                prepare_x(n + 1)
+                prepare_weights(1, n + 1)
             prepare_hidden(n)
-        quantise_weights(2, 0, regroup_weights(2, 0))
+        prepare_weights(2, 0)
         for n in range(BLOCKS):
             if n + 1 < BLOCKS:
-                quantise_weights(2, n + 1, regroup_weights(2, n + 1))
+                prepare_weights(2, n + 1)
             layer2(n)

@@ -13,7 +13,7 @@ ADD = mybir.AluOpType.add
 
 P = 128
 PACK = 4
-RUN = 4
+RUN = 2
 BATCH = 4
 BLOCKS = 4
 WIDTH = 512

@@ -20,6 +20,8 @@ WIDTH = 512
 TILES = WIDTH // P
 SPOTS = 96
 POSITIONS = BATCH * SPOTS
+LAST_TILE = (BLOCKS - 1, TILES - 1)
+STORES = (((), (slice(0, BATCH),)), ((slice(0, 2),), (slice(2, BATCH),)))
 PARTS = 2
 REAL, IMAG = 0, 1
 BIAS_ROWS = PARTS * BLOCKS * TILES
@@ -112,18 +114,24 @@ def tile_scatteringmodule_pa_kernel(tc, xh, w1, w2, b1, b2, out):
         def prepare_weights(layer, n):
             codes = weights.tile([P, PARTS, WIDTH], U32, name="w_codes%d_%d" % (layer, n), align_bytes=64)
             scales = weights.tile([P, PARTS, WIDTH], U8, name="w_scales%d_%d" % (layer, n), align_bytes=64)
+            grouped = []
             for part in range(PARTS):
-                grouped = w_stage.tile([P, WIDTH, PACK], BF16, name="w_grouped", align_bytes=64)
-                copy = nc.vector.tensor_copy if (layer == 1 and part == IMAG) else nc.scalar.copy
-                copy(
-                    out=grouped[:].rearrange("p (c i) j -> p c j i", i=RUN),
-                    in_=w_raw[(layer, n, part)][:].rearrange("p j (c i) -> p c j i", i=RUN),
-                )
-                nc.vector.quantize_mx(
-                    out=codes[:, part, :].bitcast(FP8X4),
-                    scales=scales[:, part, :],
-                    in_=grouped[:].rearrange("p c j -> p (c j)"),
-                )
+                w_tile = w_stage.tile([P, WIDTH, PACK], BF16, name="w_grouped", align_bytes=64)
+                grouped.append(w_tile)
+            step = WIDTH // 2 if (layer, n) == (2, BLOCKS - 1) else WIDTH
+            for first in range(0, WIDTH, step):
+                columns = slice(first, first + step)
+                for part in range(PARTS):
+                    copy = nc.vector.tensor_copy if (layer == 1 and part == IMAG) else nc.scalar.copy
+                    copy(
+                        out=grouped[part][:, columns, :].rearrange("p (c i) j -> p c j i", i=RUN),
+                        in_=w_raw[(layer, n, part)][:, :, columns].rearrange("p j (c i) -> p c j i", i=RUN),
+                    )
+                    nc.vector.quantize_mx(
+                        out=codes[:, part, columns].bitcast(FP8X4),
+                        scales=scales[:, part, columns],
+                        in_=grouped[part][:, columns, :].rearrange("p c j -> p (c j)"),
+                    )
             w_mx[(layer, n)] = (codes, scales)
 
         def layer1(n):
@@ -163,7 +171,11 @@ def tile_scatteringmodule_pa_kernel(tc, xh, w1, w2, b1, b2, out):
                         in1=bias2[:, n, t, :].unsqueeze(1).to_broadcast([P, count, PARTS]),
                         op=ADD,
                     )
-                nc.sync.dma_start(out=out_view[n, t], in_=result[:].rearrange("p (b q) r -> p b (q r)", b=BATCH))
+                    for entries in STORES[(n, t) == LAST_TILE][first > 0]:
+                        nc.sync.dma_start(
+                            out=out_view[n, t][:, entries],
+                            in_=result[:].rearrange("p (b q) r -> p b (q r)", b=BATCH)[:, entries],
+                        )
 
         bias_rows = const.tile([P, P], BF16)
         nc.gpsimd.memset(bias_rows[:], 0.0)

import concourse.mybir as mybir
from concourse.masks import make_identity

FLOPS = 8 * 4 * 384 * 512 * 512 * 2

BF16 = mybir.dt.bfloat16
F32 = mybir.dt.float32
U32 = mybir.dt.uint32
U8 = mybir.dt.uint8
FP8X4 = mybir.dt.float8_e4m3fn_x4
RELU = mybir.ActivationFunctionType.Relu
ADD = mybir.AluOpType.add

P = 128
PACK = 4
RUN = 2
BATCH = 4
BLOCKS = 4
WIDTH = 512
TILES = WIDTH // P
SPOTS = 96
POSITIONS = BATCH * SPOTS
LAST_TILE = (BLOCKS - 1, TILES - 1)
STORES = (((), (slice(0, BATCH),)), ((slice(0, 2),), (slice(2, BATCH),)))
PARTS = 2
REAL, IMAG = 0, 1
BIAS_ROWS = PARTS * BLOCKS * TILES

NEG, RE, IM = 0, POSITIONS, 2 * POSITIONS
SETS = 3 * POSITIONS
MOVING = ((RE, NEG), (IM, RE))
POSITION_RANGES = ((0, 256), (256, 128))
QUANTISE_RANGES = ((0, 1024), (1024, 128))


def negate_and_quantise(nc, grouped, codes, scales):
    nc.vector.tensor_scalar_mul(
        out=grouped[:, NEG : NEG + POSITIONS, :], in0=grouped[:, IM : IM + POSITIONS, :], scalar1=-1.0
    )
    for first, count in QUANTISE_RANGES:
        nc.vector.quantize_mx(
            out=codes[:, first : first + count].bitcast(FP8X4),
            scales=scales[:, first : first + count],
            in_=grouped[:, first : first + count, :].rearrange("p c j -> p (c j)"),
        )


def complex_product(nc, acc, weight, t, activation, part, first, count):
    w_codes, w_scales = weight
    a_codes, a_scales = activation
    channels = slice(t * P, (t + 1) * P)
    for w_part in range(PARTS):
        start = MOVING[part][w_part] + first
        nc.tensor.matmul_mx(
            out=acc,
            lhsT=w_codes[:, w_part, channels].bitcast(FP8X4),
            lhsT_scale=w_scales[:, w_part, channels],
            rhs=a_codes[:, start : start + count].bitcast(FP8X4),
            rhs_scale=a_scales[:, start : start + count],
            start=(w_part == 0),
            stop=(w_part == PARTS - 1),
        )


def tile_scatteringmodule_pa_kernel(tc, xh, w1, w2, b1, b2, out):
    nc = tc.nc
    x_view = xh.rearrange("b (n p j) o h w r -> n p b (j o h w r)", n=BLOCKS, p=P, j=PACK)
    out_view = out.rearrange("b (n t p) o h w r -> n t p b (o h w r)", n=BLOCKS, t=TILES, p=P)

    with (
        tc.tile_pool(name="const", bufs=1) as const,
        tc.tile_pool(name="raw", bufs=1) as raw,
        tc.tile_pool(name="w_raw_pool", bufs=12) as w_raw_pool,
        tc.tile_pool(name="hidden_mx", bufs=1) as hidden_mx,
        tc.tile_pool(name="weights", bufs=1) as weights,
        tc.tile_pool(name="stage", bufs=2) as stage,
        tc.tile_pool(name="w_stage", bufs=3) as w_stage,
        tc.tile_pool(name="results", bufs=6) as results,
        tc.psum_pool(name="psum", bufs=8) as psum,
    ):
        x_raw = {}
        w_raw = {}
        x_mx = {}
        w_mx = {}
        planes = {}
        h_mx = {}

        def load_x(n):
            x_raw[n] = raw.tile([P, BATCH, PACK, SPOTS, PARTS], BF16, name="x_raw%d" % n)
            nc.sync.dma_start(out=x_raw[n][:].rearrange("p b j q r -> p b (j q r)"), in_=x_view[n])

        def load_weights(layer, n):
            for part in range(PARTS):
                w_tile = w_raw_pool.tile([P, PACK, WIDTH], BF16, name="w_raw")
                if layer == 1:
                    rows = w1[part, n].rearrange("(p j) k -> p j k", j=PACK)
                else:
                    rows = w2[part, n].rearrange("(t p) k -> p t k", p=P)
                nc.sync.dma_start(out=w_tile[:], in_=rows)
                w_raw[(layer, n, part)] = w_tile

        def prepare_x(n):
            grouped = stage.tile([P, SETS, PACK], BF16, name="x_grouped", align_bytes=64)
            for part, first, copy in ((REAL, RE, nc.scalar.copy), (IMAG, IM, nc.vector.tensor_copy)):
                copy(
                    out=grouped[:, first : first + POSITIONS, :].rearrange("p (b c i) j -> p b c j i", b=BATCH, i=RUN),
                    in_=x_raw[n][:, :, :, :, part].rearrange("p b j (c i) -> p b c j i", i=RUN),
                )
            codes = stage.tile([P, SETS], U32, name="x_codes", align_bytes=64)
            scales = stage.tile([P, SETS], U8, name="x_scales", align_bytes=64)
            negate_and_quantise(nc, grouped, codes, scales)
            x_mx[n] = (codes, scales)

        def prepare_weights(layer, n):
            codes = weights.tile([P, PARTS, WIDTH], U32, name="w_codes%d_%d" % (layer, n), align_bytes=64)
            scales = weights.tile([P, PARTS, WIDTH], U8, name="w_scales%d_%d" % (layer, n), align_bytes=64)
            grouped = []
            for part in range(PARTS):
                w_tile = w_stage.tile([P, WIDTH, PACK], BF16, name="w_grouped", align_bytes=64)
                grouped.append(w_tile)
            step = WIDTH // 2 if (layer, n) == (2, BLOCKS - 1) else WIDTH
            for first in range(0, WIDTH, step):
                columns = slice(first, first + step)
                for part in range(PARTS):
                    copy = nc.vector.tensor_copy if (layer == 1 and part == IMAG) else nc.scalar.copy
                    copy(
                        out=grouped[part][:, columns, :].rearrange("p (c i) j -> p c j i", i=RUN),
                        in_=w_raw[(layer, n, part)][:, :, columns].rearrange("p j (c i) -> p c j i", i=RUN),
                    )
                    nc.vector.quantize_mx(
                        out=codes[:, part, columns].bitcast(FP8X4),
                        scales=scales[:, part, columns],
                        in_=grouped[part][:, columns, :].rearrange("p c j -> p (c j)"),
                    )
            w_mx[(layer, n)] = (codes, scales)

        def layer1(n):
            planes[n] = stage.tile([P, PARTS, TILES, POSITIONS], BF16, name="planes")
            for part in range(PARTS):
                for t in range(TILES):
                    hidden = psum.tile([P, POSITIONS], F32, name="hidden", tag="bank")
                    for first, count in POSITION_RANGES:
                        complex_product(nc, hidden[:, first : first + count], w_mx[(1, n)], t, x_mx[n], part, first, count)
                    nc.scalar.activation(
                        out=planes[n][:, part, t, :], in_=hidden[:], func=RELU,
                        bias=bias1[:, part, n, t : t + 1], scale=1.0,
                    )

        def prepare_hidden(n):
            grouped = stage.tile([P, SETS, PACK], BF16, name="h_grouped", align_bytes=64)
            for part, first in ((REAL, RE), (IMAG, IM)):
                nc.vector.tensor_copy(
                    out=grouped[:, first : first + POSITIONS, :].rearrange("p (c i) t -> p c t i", i=RUN),
                    in_=planes[n][:, part, :, :].rearrange("p t (c i) -> p c t i", i=RUN),
                )
            codes = hidden_mx.tile([P, SETS], U32, name="h_codes%d" % n, align_bytes=64)
            scales = hidden_mx.tile([P, SETS], U8, name="h_scales%d" % n, align_bytes=64)
            negate_and_quantise(nc, grouped, codes, scales)
            h_mx[n] = (codes, scales)

        def layer2(n):
            for t in range(TILES):
                result = results.tile([P, POSITIONS, PARTS], F32, name="result")
                for first, count in POSITION_RANGES:
                    pair = psum.tile([P, PARTS, count], F32, name="pair", tag="bank")
                    for part in range(PARTS):
                        complex_product(nc, pair[:, part, :], w_mx[(2, n)], t, h_mx[n], part, first, count)
                    nc.vector.tensor_tensor(
                        out=result[:, first : first + count, :],
                        in0=pair[:].rearrange("p r q -> p q r"),
                        in1=bias2[:, n, t, :].unsqueeze(1).to_broadcast([P, count, PARTS]),
                        op=ADD,
                    )
                    for entries in STORES[(n, t) == LAST_TILE][first > 0]:
                        nc.sync.dma_start(
                            out=out_view[n, t][:, entries],
                            in_=result[:].rearrange("p (b q) r -> p b (q r)", b=BATCH)[:, entries],
                        )

        bias_rows = const.tile([P, P], BF16)
        nc.gpsimd.memset(bias_rows[:], 0.0)
        nc.sync.dma_start(out=bias_rows[0:BIAS_ROWS, :], in_=b1.rearrange("r n (t c) -> (r n t) c", c=P))
        nc.sync.dma_start(out=bias_rows[BIAS_ROWS : 2 * BIAS_ROWS, :], in_=b2.rearrange("r n (t c) -> (r n t) c", c=P))
        for n in range(BLOCKS):
            load_x(n)
            load_weights(1, n)
        for n in range(BLOCKS):
            load_weights(2, n)

        identity = const.tile([P, P], BF16)
        make_identity(nc, identity[:])
        bias_t = psum.tile([P, P], BF16, name="bias_t", tag="bank")
        nc.tensor.transpose(out=bias_t[:], in_=bias_rows[:], identity=identity[:])
        bias1 = const.tile([P, PARTS, BLOCKS, TILES], F32)
        nc.vector.tensor_copy(out=bias1[:].rearrange("p r n t -> p (r n t)"), in_=bias_t[:, 0:BIAS_ROWS])
        bias2 = const.tile([P, BLOCKS, TILES, PARTS], F32)
        nc.vector.tensor_copy(
            out=bias2[:].rearrange("p n t r -> p (n t) r"),
            in_=bias_t[:, BIAS_ROWS : 2 * BIAS_ROWS].rearrange("p (r c) -> p c r", r=PARTS),
        )

        prepare_x(0)
        prepare_weights(1, 0)
        for n in range(BLOCKS):
            layer1(n)
            if n + 1 < BLOCKS:
                prepare_x(n + 1)
                prepare_weights(1, n + 1)
            prepare_hidden(n)
        prepare_weights(2, 0)
        for n in range(BLOCKS):
            if n + 1 < BLOCKS:
                prepare_weights(2, n + 1)
            layer2(n)
